import numpy as np
import ml_dtypes


def mxq(x, axis, fmt="e4m3"):
    dtype, down = {"e4m3": (ml_dtypes.float8_e4m3fn, 7), "e5m2": (ml_dtypes.float8_e5m2, 14)}[fmt]
    v = np.moveaxis(np.asarray(x, np.float32).astype(ml_dtypes.bfloat16).astype(np.float64), axis, -1)
    blocks = v.reshape(v.shape[:-1] + (-1, 32))
    amax = np.abs(blocks).max(-1, keepdims=True)
    byte = np.maximum(np.where(amax > 0, np.frexp(amax)[1] - 1 + 127, 0) - down, 1)
    scale = np.exp2(byte - 127.0)
    codes = (blocks / scale).astype(np.float32).astype(dtype).astype(np.float64)
    return np.moveaxis((codes * scale).reshape(v.shape), -1, axis)


WIDE = False


def mx_kscale(k):
    if not WIDE:
        return np.ones(k)
    levels = np.array([10, -10, 5, -5, 0])
    if k % 512:
        return np.exp2(np.random.permutation(np.resize(levels, k // 32))).repeat(32)
    a = np.empty((k // 512, 16))
    for p in range(k // 512):
        a[p, :8] = np.random.permutation(np.resize(levels, 8))
        for g in range(8):
            far = levels[np.abs(levels - a[p, g]) >= 10]
            a[p, g + 8] = far[np.random.randint(len(far))]
    return np.exp2(a.ravel()).repeat(32)


BF16 = ml_dtypes.bfloat16


def bf(x):
    return np.asarray(x, np.float32).astype(BF16)


def f64(x):
    return np.asarray(x).astype(np.float64)


B, L, D, CH, S, R, NL = 1, 384, 1024, 2, 8, 128, 4
EPS = 1e-6


def rmsnorm(v, w):
    return v / np.sqrt(np.mean(v * v, axis=-1, keepdims=True) + EPS) * w


def draw0():
    n = np.random.standard_normal
    t = mx_kscale(CH * D)
    return {"y": bf(n((B, L, CH * D)) * 0.9 * t),
            "x": bf(n((B, L, D))),
            "step_emb": bf(n(D) * 0.3),
            "out_proj_w": bf(n((D, CH * D)) / np.sqrt(CH * D) / t[None, :]),
            "mixer_norm_w": bf(1.0 + 0.1 * n(D)),
            "loop_norm_w": bf(1.0 + 0.1 * n(D))}


def core(y, x, step_emb, out_proj_w, mixer_norm_w, loop_norm_w):
    h = f64(x) + f64(step_emb)
    out = rmsnorm(mxq(f64(y), 2, "e4m3") @ mxq(f64(out_proj_w), 1, "e4m3").T, f64(mixer_norm_w))
    return rmsnorm(h + out, f64(loop_norm_w))


def e4m3fn_bytes(y):
    return np.clip(np.asarray(y, np.float64), -448.0, 448.0).astype(np.float32).astype(ml_dtypes.float8_e4m3fn).view(np.uint8)


def e4m3fn_values(b):
    return np.asarray(b, np.uint8).view(ml_dtypes.float8_e4m3fn).astype(np.float64)


def setup_inputs():
    d = draw0()
    x0 = np.asarray(d['out_proj_w']).astype(np.float64)
    s = (np.max(np.abs(x0), axis=(0,), keepdims=True) / 448.0).astype(np.float32)
    out = {}
    for k, v in d.items():
        if k == 'out_proj_w':
            out['out_proj_w_bytes'] = e4m3fn_bytes(x0 / s.astype(np.float64))
            out['out_proj_w_scale'] = s
        else:
            out[k] = v
    return out


def reference(y, x, step_emb, out_proj_w_bytes, out_proj_w_scale, mixer_norm_w, loop_norm_w):
    return core(y, x, step_emb, e4m3fn_values(out_proj_w_bytes) * out_proj_w_scale.astype(np.float64), mixer_norm_w, loop_norm_w)

@@ -1,0 +1,303 @@
+from contextlib import ExitStack
+
+import concourse.mybir as mybir
+from concourse.masks import make_identity
+
+F32 = mybir.dt.float32
+BF16 = mybir.dt.bfloat16
+U32 = mybir.dt.uint32
+U8 = mybir.dt.uint8
+FP8 = mybir.dt.float8_e4m3fn
+FP8X4 = mybir.dt.float8_e4m3fn_x4
+ALU = mybir.AluOpType
+ACT = mybir.ActivationFunctionType
+
+L, D, K = 384, 1024, 2048
+EPS = 1e-6
+FLOPS = 2 * L * D * K
+
+P = 128
+K_PASS = 512
+PASSES = K // K_PASS
+M_TILES = L // P
+HALF = 512
+HALVES = D // HALF
+UNITS = HALVES * PASSES
+ROW_TILES = D // P
+
+
+def tile_recursivemamba130m_pb_kernel(
+    tc, y, x, step_emb, out_proj_w_bytes, out_proj_w_scale, mixer_norm_w, loop_norm_w, out
+):
+    nc = tc.nc
+    y2 = y.flatten_outer_dims()
+    x2 = x.flatten_outer_dims()
+    out2 = out.flatten_outer_dims()
+
+    with ExitStack() as ctx:
+        keep = ctx.enter_context(tc.tile_pool(name="keep", bufs=1))
+        stream = ctx.enter_context(tc.tile_pool(name="stream", bufs=3))
+        accp = ctx.enter_context(tc.psum_pool(name="accp", bufs=1))
+        tpp = ctx.enter_context(tc.psum_pool(name="tpp", bufs=2))
+        ctx.enter_context(tc.manual_schedule())
+
+        scale4 = keep.tile([P, PASSES * 8], F32, name="scale4")
+        scale_view = out_proj_w_scale.rearrange("o (g p t) -> g p (o t)", p=P, t=4)
+
+        def load_scales(g):
+            nc.sync.dma_start(out=scale4[:, 8 * g : 8 * g + 4], in_=scale_view[g])
+
+        ident = keep.tile([P, P], F32, name="ident")
+        make_identity(nc, ident[:])
+        zero_col = keep.tile([P, 1], F32, name="zero_col")
+        nc.vector.memset(zero_col[:], 0.0)
+        eps_col = keep.tile([P, 1], F32, name="eps_col")
+        nc.vector.tensor_scalar(out=eps_col[:], in0=zero_col[:], scalar1=EPS, scalar2=None, op0=ALU.add)
+        warm_col = keep.tile([P, 1], F32, name="warm_col")
+        nc.scalar.activation(out=warm_col[:], in_=eps_col[:], func=ACT.Abs_reciprocal_sqrt)
+        ident_bf = keep.tile([P, P], BF16, name="ident_bf")
+        make_identity(nc, ident_bf[:])
+        ones_bf = keep.tile([P, P], BF16, name="ones_bf")
+        nc.gpsimd.memset(ones_bf[:], 1.0)
+        step_pad = keep.tile([P, D], BF16, name="step_pad")
+        nc.gpsimd.memset(step_pad[:], 0.0)
+
+        w_bytes = [keep.tile([P, K], U8, name="w_bytes%d" % r) for r in range(ROW_TILES)]
+        y_sb = [keep.tile([P, K], BF16, name="y_sb%d" % m) for m in range(M_TILES)]
+        x_sb = [keep.tile([P, D], BF16, name="x_sb%d" % m) for m in range(M_TILES)]
+        step_bc = keep.tile([P, D], BF16, name="step_bc")
+        w1_bc = keep.tile([P, D], BF16, name="w1_bc")
+        w2_bc = keep.tile([P, D], BF16, name="w2_bc")
+
+        def load_w(r):
+            nc.sync.dma_start(out=w_bytes[r][:], in_=out_proj_w_bytes[r * P : (r + 1) * P, :])
+
+        for r in range(4):
+            nc.sync.dma_start(out=w_bytes[r][:, :K_PASS], in_=out_proj_w_bytes[r * P : (r + 1) * P, :K_PASS])
+        load_scales(0)
+        for r in range(4):
+            nc.sync.dma_start(out=w_bytes[r][:, K_PASS:], in_=out_proj_w_bytes[r * P : (r + 1) * P, K_PASS:])
+        for g in range(1, PASSES):
+            load_scales(g)
+        for m in range(M_TILES):
+            nc.sync.dma_start(out=y_sb[m][:], in_=y2[m * P : (m + 1) * P, :])
+        for r in range(4, 8):
+            load_w(r)
+        nc.sync.dma_start(out=step_pad[0:1, :], in_=step_emb.rearrange("(o d) -> o d", o=1))
+        for m in range(M_TILES):
+            nc.sync.dma_start(out=x_sb[m][:], in_=x2[m * P : (m + 1) * P, :])
+        nc.sync.dma_start(out=w1_bc[:], in_=mixer_norm_w.partition_broadcast(P))
+        nc.sync.dma_start(out=step_bc[:], in_=step_emb.partition_broadcast(P))
+        nc.sync.dma_start(out=w2_bc[:], in_=loop_norm_w.partition_broadcast(P))
+
+        y_codes = [keep.tile([P, PASSES * P], U32, name="y_codes%d" % m, align_bytes=64) for m in range(M_TILES)]
+        y_scales = [keep.tile([P, PASSES * P], U8, name="y_scales%d" % m, align_bytes=64) for m in range(M_TILES)]
+        w_codes = [keep.tile([P, HALF], U32, name="w_codes%d" % u, align_bytes=64) for u in range(UNITS)]
+        w_scales = [keep.tile([P, HALF], U8, name="w_scales%d" % u, align_bytes=64) for u in range(UNITS)]
+        h_last = keep.tile([P, D], F32, name="h_last")
+        h_banks = {}
+        pw_sb = [keep.tile([P, D], F32, name="pw_sb%d" % m) for m in range(M_TILES)]
+        z_sb = [keep.tile([P, D], F32, name="z_sb%d" % m) for m in range(M_TILES)]
+        res_sb = [keep.tile([P, D], F32, name="res_sb%d" % m) for m in range(M_TILES)]
+        ss_p = [[keep.tile([P, 1], F32, name="ss_p%d_%d" % (m, hf)) for hf in range(HALVES)] for m in range(M_TILES)]
+        bias_a = [keep.tile([P, 1], F32, name="bias_a%d" % m) for m in range(M_TILES)]
+        r1 = [keep.tile([P, 1], F32, name="r1_%d" % m) for m in range(M_TILES)]
+        ss_z = [keep.tile([P, 1], F32, name="ss_z%d" % m) for m in range(M_TILES)]
+        r2 = [keep.tile([P, 1], F32, name="r2_%d" % m) for m in range(M_TILES)]
+        acc = {}
+
+        def turn_bank(bank, word_blocks):
+            for jj in range(2):
+                for uu in range(2):
+                    nc.tensor.transpose(
+                        bank[:, uu * 256 + jj * P : uu * 256 + (jj + 1) * P], word_blocks[jj][:, uu : 2 * P : 2], ident[:]
+                    )
+
+        y_grouped = [stream.tile([P, K], BF16, name="y_grouped", align_bytes=64) for m in range(M_TILES)]
+        y_banks = {}
+
+        def turn_y(m, b):
+            bank = accp.tile([P, 512], F32, name="y_bank", tag="late%d" % ((2 * m + b) % 3))
+            words = y_sb[m][:].bitcast(F32)
+            turn_bank(bank, [words[:, (2 * b + jj) * 256 : (2 * b + jj + 1) * 256] for jj in range(2)])
+            y_banks[(m, b)] = bank
+
+        def empty_y(m, b):
+            nc.scalar.copy(
+                out=y_grouped[m][:].bitcast(F32)[:, b * 512 : (b + 1) * 512].rearrange("p (r u) -> p r u", u=2),
+                in_=y_banks[(m, b)][:].rearrange("p (u r) -> p r u", u=2),
+            )
+
+        def quantize_y(m):
+            nc.vector.quantize_mx(out=y_codes[m][:].bitcast(FP8X4), scales=y_scales[m][:], in_=y_grouped[m][:])
+
+        w_wide = {}
+        w_banks = {}
+        w_grouped = {}
+
+        def widen(u, on_vector):
+            hf, g = divmod(u, PASSES)
+            wide = stream.tile([P, 4, K_PASS], BF16, name="w_wide")
+            for j in range(4):
+                src = w_bytes[4 * hf + j][:, g * K_PASS : (g + 1) * K_PASS].bitcast(FP8)
+                if on_vector:
+                    nc.vector.tensor_copy(out=wide[:, j, :], in_=src)
+                else:
+                    nc.scalar.copy(out=wide[:, j, :], in_=src)
+            w_wide[u] = wide
+
+        def turn_w(u, b, bank=None):
+            if bank is None:
+                bank = tpp.tile([P, 512], F32, name="w_bank")
+            turn_bank(bank, [w_wide[u][:, 2 * b + jj, :].bitcast(F32) for jj in range(2)])
+            w_banks[(u, b)] = bank
+
+        def scale_w(u, b):
+            g = u % PASSES
+            if u not in w_grouped:
+                w_grouped[u] = stream.tile([P, 4 * HALF], BF16, name="w_grouped", align_bytes=64)
+            nc.vector.tensor_tensor(
+                out=w_grouped[u][:, b * 1024 : (b + 1) * 1024].rearrange("p (r u e) -> p r u e", u=2, e=2),
+                in0=w_banks[(u, b)][:].bitcast(BF16).rearrange("p (u r e) -> p r u e", u=2, e=2),
+                in1=scale4[:, 8 * g : 8 * g + 4].rearrange("p (u e) -> p u e", u=2).unsqueeze(1).to_broadcast([P, 256, 2, 2]),
+                op=ALU.mult,
+            )
+
+        def scale_w_on_scalar(u, b):
+            g = u % PASSES
+            w_grouped[u] = stream.tile([P, 4 * HALF], BF16, name="w_grouped", align_bytes=64)
+            planes_out = w_grouped[u][:, b * 1024 : (b + 1) * 1024].rearrange("p (r t) -> p r t", t=4)
+            planes_in = w_banks[(u, b)][:].bitcast(BF16).rearrange("p (u r e) -> p u r e", u=2, e=2)
+            for t in range(4):
+                nc.scalar.activation(
+                    out=planes_out[:, :, t], in_=planes_in[:, t // 2, :, t % 2], func=ACT.Copy,
+                    scale=scale4[:, 8 * g + t : 8 * g + t + 1],
+                )
+
+        def quantize_w(u):
+            nc.vector.quantize_mx(out=w_codes[u][:].bitcast(FP8X4), scales=w_scales[u][:], in_=w_grouped[u][:])
+
+        def multiply(u, m):
+            hf, g = divmod(u, PASSES)
+            if g == 0:
+                acc[(m, hf)] = accp.tile([P, HALF], F32, name="acc", tag=("early%d" if hf == 0 else "late%d") % m)
+            nc.tensor.matmul_mx(
+                out=acc[(m, hf)][:],
+                lhsT=y_codes[m][:, g * P : (g + 1) * P].bitcast(FP8X4),
+                lhsT_scale=y_scales[m][:, g * P : (g + 1) * P],
+                rhs=w_codes[u][:].bitcast(FP8X4),
+                rhs_scale=w_scales[u][:],
+                start=(g == 0),
+                stop=(g == PASSES - 1),
+            )
+
+        def residual_on_tensor(m, hf, bank):
+            cols = slice(hf * HALF, (hf + 1) * HALF)
+            nc.tensor.matmul(out=bank[:], lhsT=ident_bf[:], rhs=x_sb[m][:, cols], start=True, stop=False)
+            nc.tensor.matmul(out=bank[:], lhsT=ones_bf[:], rhs=step_pad[:, cols], start=False, stop=True)
+            h_banks[(m, hf)] = bank
+
+        def square_p(m, hf):
+            junk = stream.tile([P, HALF], F32, name="junk_p")
+            nc.scalar.activation(out=junk[:], in_=acc[(m, hf)][:], func=ACT.Square, accum_out=ss_p[m][hf][:])
+
+        def gain_p(m, hf):
+            cols = slice(hf * HALF, (hf + 1) * HALF)
+            nc.vector.tensor_tensor(out=pw_sb[m][:, cols], in0=acc[(m, hf)][:], in1=w1_bc[:, cols], op=ALU.mult)
+
+        def residual_last():
+            nc.vector.tensor_tensor(out=h_last[:], in0=x_sb[M_TILES - 1][:], in1=step_bc[:], op=ALU.add)
+
+        def first_bias(m):
+            nc.gpsimd.tensor_scalar(
+                out=bias_a[m][:], in0=ss_p[m][0][:], scalar1=1.0 / D, scalar2=EPS, op0=ALU.mult, op1=ALU.add
+            )
+
+        def first_root(m):
+            nc.scalar.activation(
+                out=r1[m][:], in_=ss_p[m][1][:], func=ACT.Abs_reciprocal_sqrt, bias=bias_a[m][:], scale=1.0 / D
+            )
+
+        def first_norm(m):
+            if m == M_TILES - 1:
+                nc.vector.scalar_tensor_tensor(
+                    out=z_sb[m][:], in0=pw_sb[m][:], scalar=r1[m][:], in1=h_last[:], op0=ALU.mult, op1=ALU.add
+                )
+            else:
+                for hf in range(HALVES):
+                    cols = slice(hf * HALF, (hf + 1) * HALF)
+                    nc.vector.scalar_tensor_tensor(
+                        out=z_sb[m][:, cols], in0=pw_sb[m][:, cols], scalar=r1[m][:], in1=h_banks[(m, hf)][:],
+                        op0=ALU.mult, op1=ALU.add,
+                    )
+
+        def second_root(m):
+            junk = stream.tile([P, D], F32, name="junk_z")
+            nc.scalar.activation(out=junk[:], in_=z_sb[m][:], func=ACT.Square, accum_out=ss_z[m][:])
+            nc.scalar.activation(
+                out=r2[m][:], in_=ss_z[m][:], func=ACT.Abs_reciprocal_sqrt, bias=eps_col[:], scale=1.0 / D
+            )
+
+        def second_norm(m):
+            for hf in range(HALVES):
+                cols = slice(hf * HALF, (hf + 1) * HALF)
+                nc.vector.scalar_tensor_tensor(
+                    out=res_sb[m][:, cols], in0=z_sb[m][:, cols], scalar=r2[m][:], in1=w2_bc[:, cols],
+                    op0=ALU.mult, op1=ALU.mult,
+                )
+                nc.sync.dma_start(out=out2[m * P : (m + 1) * P, cols], in_=res_sb[m][:, cols])
+
+        widen(0, True)
+        widen(1, False)
+        turn_w(0, 0)
+        turn_w(0, 1)
+        for u in range(UNITS):
+            scale_w(u, 0)
+            if u == 7:
+                residual_on_tensor(1, 1, tpp.tile([P, HALF], F32, name="w_bank"))
+            if u + 1 < UNITS:
+                turn_w(u + 1, 0)
+            if u < 7:
+                scale_w(u, 1)
+            if u + 2 < UNITS:
+                widen(u + 2, False)
+            if u + 1 < 7:
+                turn_w(u + 1, 1)
+            if u >= 1:
+                quantize_w(u - 1)
+            if u < M_TILES:
+                for b in range(2):
+                    turn_y(u, b)
+                    empty_y(u, b)
+            if 1 <= u <= M_TILES:
+                quantize_y(u - 1)
+            for v in range(u):
+                for m in range(min(u, M_TILES)):
+                    if v == u - 1 or m == u - 1:
+                        multiply(v, m)
+            if u == 4:
+                for m in range(M_TILES):
+                    square_p(m, 0)
+            if u == 5:
+                for m in range(M_TILES):
+                    gain_p(m, 0)
+                    first_bias(m)
+                turn_w(7, 1, accp.tile([P, HALF], F32, name="s_bank", tag="early0"))
+                scale_w_on_scalar(7, 1)
+                for hf in range(HALVES):
+                    residual_on_tensor(0, hf, accp.tile([P, HALF], F32, name="h_bank", tag="early%d" % (hf + 1)))
+            if u == 6:
+                residual_on_tensor(1, 0, tpp.tile([P, HALF], F32, name="w_bank"))
+        quantize_w(UNITS - 1)
+        for m in range(M_TILES):
+            multiply(UNITS - 1, m)
+        residual_last()
+        for m in range(M_TILES):
+            square_p(m, 1)
+            first_root(m)
+            gain_p(m, 1)
+        for m in range(M_TILES):
+            first_norm(m)
+            second_root(m)
+        for m in range(M_TILES):
+            second_norm(m)

@@ -135,16 +135,26 @@ def tile_recursivemamba130m_pb_kernel(
         w_banks = {}
         w_grouped = {}
 
-        def widen(u, on_vector):
+        def widen(u, on_vector, on_gpsimd=0):
             hf, g = divmod(u, PASSES)
             wide = stream.tile([P, 4, K_PASS], BF16, name="w_wide")
-            for j in range(4):
+            for j in range(4 - on_gpsimd):
                 src = w_bytes[4 * hf + j][:, g * K_PASS : (g + 1) * K_PASS].bitcast(FP8)
                 if on_vector:
                     nc.vector.tensor_copy(out=wide[:, j, :], in_=src)
                 else:
                     nc.scalar.copy(out=wide[:, j, :], in_=src)
             w_wide[u] = wide
+
+        def widen_on_gpsimd(u, j):
+            hf, g = divmod(u, PASSES)
+            src = w_bytes[4 * hf + j][:, g * K_PASS : (g + 1) * K_PASS].bitcast(FP8)
+            nc.gpsimd.tensor_copy(out=w_wide[u][:, j, :], in_=src)
+
+        g_sync = keep.tile([P, 1], U32, name="g_sync")
+
+        def gpsimd_waits_for(codes):
+            nc.gpsimd.tensor_copy(out=g_sync[:], in_=codes[:, 0:1])
 
         def turn_w(u, b, bank=None):
             if bank is None:
@@ -205,8 +215,9 @@ def tile_recursivemamba130m_pb_kernel(
             cols = slice(hf * HALF, (hf + 1) * HALF)
             nc.vector.tensor_tensor(out=pw_sb[m][:, cols], in0=acc[(m, hf)][:], in1=w1_bc[:, cols], op=ALU.mult)
 
-        def residual_last():
-            nc.vector.tensor_tensor(out=h_last[:], in0=x_sb[M_TILES - 1][:], in1=step_bc[:], op=ALU.add)
+        def residual_last(hf):
+            cols = slice(hf * HALF, (hf + 1) * HALF)
+            nc.gpsimd.tensor_tensor(out=h_last[:, cols], in0=x_sb[M_TILES - 1][:, cols], in1=step_bc[:, cols], op=ALU.add)
 
         def first_bias(m):
             nc.gpsimd.tensor_scalar(
@@ -260,7 +271,7 @@ def tile_recursivemamba130m_pb_kernel(
             if u < 7:
                 scale_w(u, 1)
             if u + 2 < UNITS:
-                widen(u + 2, False)
+                widen(u + 2, False, 1)
             if u + 1 < 7:
                 turn_w(u + 1, 1)
             if u >= 1:
@@ -271,6 +282,10 @@ def tile_recursivemamba130m_pb_kernel(
                     empty_y(u, b)
             if 1 <= u <= M_TILES:
                 quantize_y(u - 1)
+            if 1 <= u < UNITS - 2:
+                gpsimd_waits_for(y_codes[u - 1] if u <= M_TILES else w_codes[u - 1])
+            if u + 2 < UNITS:
+                widen_on_gpsimd(u + 2, 3)
             for v in range(u):
                 for m in range(min(u, M_TILES)):
                     if v == u - 1 or m == u - 1:
@@ -279,6 +294,8 @@ def tile_recursivemamba130m_pb_kernel(
                 for m in range(M_TILES):
                     square_p(m, 0)
             if u == 5:
+                for hf in range(HALVES):
+                    residual_last(hf)
                 for m in range(M_TILES):
                     gain_p(m, 0)
                     first_bias(m)
@@ -291,7 +308,6 @@ def tile_recursivemamba130m_pb_kernel(
         quantize_w(UNITS - 1)
         for m in range(M_TILES):
             multiply(UNITS - 1, m)
-        residual_last()
         for m in range(M_TILES):
             square_p(m, 1)
             first_root(m)

@@ -264,8 +264,6 @@ def tile_recursivemamba130m_pb_kernel(
         turn_w(0, 1)
         for u in range(UNITS):
             scale_w(u, 0)
-            if u == 7:
-                residual_on_tensor(1, 1, tpp.tile([P, HALF], F32, name="w_bank"))
             if u + 1 < UNITS:
                 turn_w(u + 1, 0)
             if u < 7:
@@ -308,12 +306,18 @@ def tile_recursivemamba130m_pb_kernel(
         quantize_w(UNITS - 1)
         for m in range(M_TILES):
             multiply(UNITS - 1, m)
-        for m in range(M_TILES):
-            square_p(m, 1)
-            first_root(m)
-            gain_p(m, 1)
-        for m in range(M_TILES):
+        residual_on_tensor(1, 1, tpp.tile([P, HALF], F32, name="w_bank"))
+        gain_p(0, 1)
+        square_p(1, 1)
+        first_root(1)
+        gain_p(1, 1)
+        square_p(0, 1)
+        first_root(0)
+        gain_p(2, 1)
+        square_p(2, 1)
+        first_root(2)
+        for m in (1, 0, 2):
             first_norm(m)
             second_root(m)
-        for m in range(M_TILES):
+        for m in (1, 0, 2):
             second_norm(m)

@@ -58,9 +58,9 @@ def tile_recursivemamba130m_pb_kernel(
         ident_bf = keep.tile([P, P], BF16, name="ident_bf")
         make_identity(nc, ident_bf[:])
         ones_bf = keep.tile([P, P], BF16, name="ones_bf")
-        nc.gpsimd.memset(ones_bf[:], 1.0)
+        nc.vector.memset(ones_bf[:], 1.0)
         step_pad = keep.tile([P, D], BF16, name="step_pad")
-        nc.gpsimd.memset(step_pad[:], 0.0)
+        nc.vector.memset(step_pad[:], 0.0)
 
         w_bytes = [keep.tile([P, K], U8, name="w_bytes%d" % r) for r in range(ROW_TILES)]
         y_sb = [keep.tile([P, K], BF16, name="y_sb%d" % m) for m in range(M_TILES)]

@@ -86,23 +86,25 @@ def tile_recursivemamba130m_pb_kernel(
         nc.sync.dma_start(out=step_pad[0:1, :], in_=step_emb.rearrange("(o d) -> o d", o=1))
         for m in range(M_TILES):
             nc.sync.dma_start(out=x_sb[m][:], in_=x2[m * P : (m + 1) * P, :])
-        nc.sync.dma_start(out=w1_bc[:], in_=mixer_norm_w.partition_broadcast(P))
         nc.sync.dma_start(out=step_bc[:], in_=step_emb.partition_broadcast(P))
+        nc.sync.dma_start(out=w1_bc[:], in_=mixer_norm_w.partition_broadcast(P))
         nc.sync.dma_start(out=w2_bc[:], in_=loop_norm_w.partition_broadcast(P))
 
         y_codes = [keep.tile([P, PASSES * P], U32, name="y_codes%d" % m, align_bytes=64) for m in range(M_TILES)]
         y_scales = [keep.tile([P, PASSES * P], U8, name="y_scales%d" % m, align_bytes=64) for m in range(M_TILES)]
         w_codes = [keep.tile([P, HALF], U32, name="w_codes%d" % u, align_bytes=64) for u in range(UNITS)]
         w_scales = [keep.tile([P, HALF], U8, name="w_scales%d" % u, align_bytes=64) for u in range(UNITS)]
-        h_last = keep.tile([P, D], F32, name="h_last")
+        h_sb = [keep.tile([P, D], F32, name="h_sb%d" % m) for m in range(2)]
         h_banks = {}
+        diag_r1 = keep.tile([P, P], F32, name="diag_r1")
         pw_sb = [keep.tile([P, D], F32, name="pw_sb%d" % m) for m in range(M_TILES)]
         z_sb = [keep.tile([P, D], F32, name="z_sb%d" % m) for m in range(M_TILES)]
         res_sb = [keep.tile([P, D], F32, name="res_sb%d" % m) for m in range(M_TILES)]
         ss_p = [[keep.tile([P, 1], F32, name="ss_p%d_%d" % (m, hf)) for hf in range(HALVES)] for m in range(M_TILES)]
         bias_a = [keep.tile([P, 1], F32, name="bias_a%d" % m) for m in range(M_TILES)]
         r1 = [keep.tile([P, 1], F32, name="r1_%d" % m) for m in range(M_TILES)]
-        ss_z = [keep.tile([P, 1], F32, name="ss_z%d" % m) for m in range(M_TILES)]
+        ss_z = [[keep.tile([P, 1], F32, name="ss_z%d_%d" % (m, hf)) for hf in range(HALVES)] for m in range(M_TILES)]
+        bias_z = [keep.tile([P, 1], F32, name="bias_z%d" % m) for m in range(M_TILES)]
         r2 = [keep.tile([P, 1], F32, name="r2_%d" % m) for m in range(M_TILES)]
         acc = {}
 
@@ -135,21 +137,18 @@ def tile_recursivemamba130m_pb_kernel(
         w_banks = {}
         w_grouped = {}
 
-        def widen(u, on_vector, on_gpsimd=0):
+        def widen(u, pieces, engine):
             hf, g = divmod(u, PASSES)
-            wide = stream.tile([P, 4, K_PASS], BF16, name="w_wide")
-            for j in range(4 - on_gpsimd):
+            if u not in w_wide:
+                w_wide[u] = stream.tile([P, 4, K_PASS], BF16, name="w_wide", bufs=4)
+            for j in pieces:
                 src = w_bytes[4 * hf + j][:, g * K_PASS : (g + 1) * K_PASS].bitcast(FP8)
-                if on_vector:
-                    nc.vector.tensor_copy(out=wide[:, j, :], in_=src)
+                if engine == "vector":
+                    nc.vector.tensor_copy(out=w_wide[u][:, j, :], in_=src)
+                elif engine == "gpsimd":
+                    nc.gpsimd.tensor_copy(out=w_wide[u][:, j, :], in_=src)
                 else:
-                    nc.scalar.copy(out=wide[:, j, :], in_=src)
-            w_wide[u] = wide
-
-        def widen_on_gpsimd(u, j):
-            hf, g = divmod(u, PASSES)
-            src = w_bytes[4 * hf + j][:, g * K_PASS : (g + 1) * K_PASS].bitcast(FP8)
-            nc.gpsimd.tensor_copy(out=w_wide[u][:, j, :], in_=src)
+                    nc.scalar.copy(out=w_wide[u][:, j, :], in_=src)
 
         g_sync = keep.tile([P, 1], U32, name="g_sync")
 
@@ -165,7 +164,7 @@ def tile_recursivemamba130m_pb_kernel(
         def scale_w(u, b):
             g = u % PASSES
             if u not in w_grouped:
-                w_grouped[u] = stream.tile([P, 4 * HALF], BF16, name="w_grouped", align_bytes=64)
+                w_grouped[u] = stream.tile([P, 4 * HALF], BF16, name="w_grouped", align_bytes=64, bufs=4)
             nc.vector.tensor_tensor(
                 out=w_grouped[u][:, b * 1024 : (b + 1) * 1024].rearrange("p (r u e) -> p r u e", u=2, e=2),
                 in0=w_banks[(u, b)][:].bitcast(BF16).rearrange("p (u r e) -> p r u e", u=2, e=2),
@@ -175,7 +174,8 @@ def tile_recursivemamba130m_pb_kernel(
 
         def scale_w_on_scalar(u, b):
             g = u % PASSES
-            w_grouped[u] = stream.tile([P, 4 * HALF], BF16, name="w_grouped", align_bytes=64)
+            if u not in w_grouped:
+                w_grouped[u] = stream.tile([P, 4 * HALF], BF16, name="w_grouped", align_bytes=64, bufs=4)
             planes_out = w_grouped[u][:, b * 1024 : (b + 1) * 1024].rearrange("p (r t) -> p r t", t=4)
             planes_in = w_banks[(u, b)][:].bitcast(BF16).rearrange("p (u r e) -> p u r e", u=2, e=2)
             for t in range(4):
@@ -201,23 +201,32 @@ def tile_recursivemamba130m_pb_kernel(
                 stop=(g == PASSES - 1),
             )
 
-        def residual_on_tensor(m, hf, bank):
+        def residual_on_tensor(m, hf, bank, more=False):
             cols = slice(hf * HALF, (hf + 1) * HALF)
             nc.tensor.matmul(out=bank[:], lhsT=ident_bf[:], rhs=x_sb[m][:, cols], start=True, stop=False)
-            nc.tensor.matmul(out=bank[:], lhsT=ones_bf[:], rhs=step_pad[:, cols], start=False, stop=True)
+            nc.tensor.matmul(out=bank[:], lhsT=ones_bf[:], rhs=step_pad[:, cols], start=False, stop=not more)
             h_banks[(m, hf)] = bank
 
         def square_p(m, hf):
             junk = stream.tile([P, HALF], F32, name="junk_p")
             nc.scalar.activation(out=junk[:], in_=acc[(m, hf)][:], func=ACT.Square, accum_out=ss_p[m][hf][:])
 
+        p_sb = [keep.tile([P, HALF], F32, name="p_sb%d" % m) for m in range(2)]
+
+        def gain_p_on_gpsimd(m, hf):
+            cols = slice(hf * HALF, (hf + 1) * HALF)
+            nc.gpsimd.tensor_tensor(out=pw_sb[m][:, cols], in0=p_sb[m][:], in1=w1_bc[:, cols], op=ALU.mult)
+
+        def copy_p(m, hf):
+            nc.scalar.copy(out=p_sb[m][:], in_=acc[(m, hf)][:])
+
         def gain_p(m, hf):
             cols = slice(hf * HALF, (hf + 1) * HALF)
             nc.vector.tensor_tensor(out=pw_sb[m][:, cols], in0=acc[(m, hf)][:], in1=w1_bc[:, cols], op=ALU.mult)
 
-        def residual_last(hf):
+        def residual_on_gpsimd(m, hf):
             cols = slice(hf * HALF, (hf + 1) * HALF)
-            nc.gpsimd.tensor_tensor(out=h_last[:, cols], in0=x_sb[M_TILES - 1][:, cols], in1=step_bc[:, cols], op=ALU.add)
+            nc.gpsimd.tensor_tensor(out=h_sb[m][:, cols], in0=x_sb[m][:, cols], in1=step_bc[:, cols], op=ALU.add)
 
         def first_bias(m):
             nc.gpsimd.tensor_scalar(
@@ -229,48 +238,106 @@ def tile_recursivemamba130m_pb_kernel(
                 out=r1[m][:], in_=ss_p[m][1][:], func=ACT.Abs_reciprocal_sqrt, bias=bias_a[m][:], scale=1.0 / D
             )
 
-        def first_norm(m):
-            if m == M_TILES - 1:
-                nc.vector.scalar_tensor_tensor(
-                    out=z_sb[m][:], in0=pw_sb[m][:], scalar=r1[m][:], in1=h_last[:], op0=ALU.mult, op1=ALU.add
-                )
-            else:
-                for hf in range(HALVES):
-                    cols = slice(hf * HALF, (hf + 1) * HALF)
-                    nc.vector.scalar_tensor_tensor(
-                        out=z_sb[m][:, cols], in0=pw_sb[m][:, cols], scalar=r1[m][:], in1=h_banks[(m, hf)][:],
-                        op0=ALU.mult, op1=ALU.add,
-                    )
-
-        def second_root(m):
-            junk = stream.tile([P, D], F32, name="junk_z")
-            nc.scalar.activation(out=junk[:], in_=z_sb[m][:], func=ACT.Square, accum_out=ss_z[m][:])
-            nc.scalar.activation(
-                out=r2[m][:], in_=ss_z[m][:], func=ACT.Abs_reciprocal_sqrt, bias=eps_col[:], scale=1.0 / D
+        def first_norm(m, hf):
+            cols = slice(hf * HALF, (hf + 1) * HALF)
+            h = h_banks[(m, hf)][:] if (m, hf) in h_banks else h_sb[m][:, cols]
+            nc.vector.scalar_tensor_tensor(
+                out=z_sb[m][:, cols], in0=pw_sb[m][:, cols], scalar=r1[m][:], in1=h, op0=ALU.mult, op1=ALU.add
             )
 
-        def second_norm(m):
-            for hf in range(HALVES):
-                cols = slice(hf * HALF, (hf + 1) * HALF)
-                nc.vector.scalar_tensor_tensor(
-                    out=res_sb[m][:, cols], in0=z_sb[m][:, cols], scalar=r2[m][:], in1=w2_bc[:, cols],
-                    op0=ALU.mult, op1=ALU.mult,
-                )
-                nc.sync.dma_start(out=out2[m * P : (m + 1) * P, cols], in_=res_sb[m][:, cols])
+        def diagonal(m):
+            nc.vector.tensor_scalar(out=diag_r1[:], in0=ident[:], scalar1=r1[m][:], scalar2=None, op0=ALU.mult)
 
-        widen(0, True)
-        widen(1, False)
-        turn_w(0, 0)
+        def first_norm_on_tensor(m, hf):
+            cols = slice(hf * HALF, (hf + 1) * HALF)
+            nc.tensor.matmul(
+                out=h_banks[(m, hf)][:], lhsT=diag_r1[:], rhs=pw_sb[m][:, cols], start=False, stop=True
+            )
+
+        def z_of(m, hf):
+            cols = slice(hf * HALF, (hf + 1) * HALF)
+            return h_banks[(m, hf)][:] if m == 2 else z_sb[m][:, cols]
+
+        def square_z(m, hf):
+            junk = stream.tile([P, HALF], F32, name="junk_p")
+            nc.scalar.activation(out=junk[:], in_=z_of(m, hf), func=ACT.Square, accum_out=ss_z[m][hf][:])
+            if hf == 0:
+                nc.gpsimd.tensor_scalar(
+                    out=bias_z[m][:], in0=ss_z[m][0][:], scalar1=1.0 / D, scalar2=EPS, op0=ALU.mult, op1=ALU.add
+                )
+            else:
+                nc.scalar.activation(
+                    out=r2[m][:], in_=ss_z[m][1][:], func=ACT.Abs_reciprocal_sqrt, bias=bias_z[m][:], scale=1.0 / D
+                )
+
+        def second_norm(m, hf):
+            cols = slice(hf * HALF, (hf + 1) * HALF)
+            nc.vector.scalar_tensor_tensor(
+                out=res_sb[m][:, cols], in0=z_of(m, hf), scalar=r2[m][:], in1=w2_bc[:, cols], op0=ALU.mult, op1=ALU.mult
+            )
+            nc.sync.dma_start(out=out2[m * P : (m + 1) * P, cols], in_=res_sb[m][:, cols])
+
+        half_banks = {}
+
+        def turn_half(u, j):
+            bank = accp.tile([P, 256], F32, name="half_bank", tag="early%d" % j)
+            for uu in range(2):
+                nc.tensor.transpose(
+                    bank[:, uu * P : (uu + 1) * P], w_wide[u][:, j, :].bitcast(F32)[:, uu : 2 * P : 2], ident[:]
+                )
+            half_banks[(u, j)] = bank
+
+        def scale_half(u, j):
+            g = u % PASSES
+            if u not in w_grouped:
+                w_grouped[u] = stream.tile([P, 4 * HALF], BF16, name="w_grouped", align_bytes=64, bufs=4)
+            nc.vector.tensor_tensor(
+                out=w_grouped[u][:, j * 512 : (j + 1) * 512].rearrange("p (r u e) -> p r u e", u=2, e=2),
+                in0=half_banks[(u, j)][:].bitcast(BF16).rearrange("p (u r e) -> p r u e", u=2, e=2),
+                in1=scale4[:, 8 * g : 8 * g + 4].rearrange("p (u e) -> p u e", u=2).unsqueeze(1).to_broadcast([P, P, 2, 2]),
+                op=ALU.mult,
+            )
+
+        def gain_z(m, hf):
+            cols = slice(hf * HALF, (hf + 1) * HALF)
+            nc.vector.tensor_tensor(out=z2_sb[:], in0=z_of(m, hf), in1=w2_bc[:, cols], op=ALU.mult)
+
+        z2_sb = keep.tile([P, HALF], F32, name="z2_sb")
+
+        def second_norm_on_scalar(m, hf):
+            cols = slice(hf * HALF, (hf + 1) * HALF)
+            nc.scalar.activation(out=res_sb[m][:, cols], in_=z2_sb[:], func=ACT.Copy, scale=r2[m][:])
+            nc.sync.dma_start(out=out2[m * P : (m + 1) * P, cols], in_=res_sb[m][:, cols])
+
+        widen(0, (0, 1, 2), "vector")
+        widen(0, (3,), "scalar")
+        turn_half(0, 0)
+        turn_half(0, 1)
         turn_w(0, 1)
-        for u in range(UNITS):
-            scale_w(u, 0)
-            if u + 1 < UNITS:
-                turn_w(u + 1, 0)
-            if u < 7:
-                scale_w(u, 1)
-            if u + 2 < UNITS:
-                widen(u + 2, False, 1)
-            if u + 1 < 7:
+        widen(1, (0, 1, 2, 3), "scalar")
+        for u in range(UNITS - 1):
+            if u == 0:
+                scale_half(0, 0)
+                scale_half(0, 1)
+            else:
+                scale_w(u, 0)
+            turn_w(u + 1, 0)
+            if u == 5:
+                turn_w(7, 1, accp.tile([P, HALF], F32, name="s_bank", tag="early0"))
+                scale_w_on_scalar(7, 1)
+                square_p(1, 0)
+                square_p(2, 0)
+            scale_w(u, 1)
+            if u == 0:
+                widen(2, (0, 1, 2), "scalar")
+                widen(2, (3,), "gpsimd")
+                widen(3, (3,), "gpsimd")
+            elif u <= 3:
+                widen(u + 2, (0, 1, 2), "scalar")
+            elif u == 4:
+                widen(6, (0, 1, 2, 3), "scalar")
+                widen(7, (2, 3, 0, 1), "scalar")
+            if u < 6:
                 turn_w(u + 1, 1)
             if u >= 1:
                 quantize_w(u - 1)
@@ -280,44 +347,60 @@ def tile_recursivemamba130m_pb_kernel(
                     empty_y(u, b)
             if 1 <= u <= M_TILES:
                 quantize_y(u - 1)
-            if 1 <= u < UNITS - 2:
+            if u >= 1:
                 gpsimd_waits_for(y_codes[u - 1] if u <= M_TILES else w_codes[u - 1])
-            if u + 2 < UNITS:
-                widen_on_gpsimd(u + 2, 3)
+            if u in (1, 2):
+                widen(u + 3, (3,), "gpsimd")
+            if 3 <= u <= 5:
+                residual_on_gpsimd(*((1, 0), (1, 1), (0, 1))[u - 3])
             for v in range(u):
                 for m in range(min(u, M_TILES)):
                     if v == u - 1 or m == u - 1:
                         multiply(v, m)
             if u == 4:
-                for m in range(M_TILES):
-                    square_p(m, 0)
+                copy_p(0, 0)
+                square_p(0, 0)
             if u == 5:
-                for hf in range(HALVES):
-                    residual_last(hf)
-                for m in range(M_TILES):
-                    gain_p(m, 0)
-                    first_bias(m)
-                turn_w(7, 1, accp.tile([P, HALF], F32, name="s_bank", tag="early0"))
-                scale_w_on_scalar(7, 1)
-                for hf in range(HALVES):
-                    residual_on_tensor(0, hf, accp.tile([P, HALF], F32, name="h_bank", tag="early%d" % (hf + 1)))
+                first_bias(0)
             if u == 6:
-                residual_on_tensor(1, 0, tpp.tile([P, HALF], F32, name="w_bank"))
-        quantize_w(UNITS - 1)
-        for m in range(M_TILES):
-            multiply(UNITS - 1, m)
-        residual_on_tensor(1, 1, tpp.tile([P, HALF], F32, name="w_bank"))
-        gain_p(0, 1)
-        square_p(1, 1)
-        first_root(1)
-        gain_p(1, 1)
-        square_p(0, 1)
-        first_root(0)
-        gain_p(2, 1)
+                gain_p_on_gpsimd(0, 0)
+                first_bias(1)
+                first_bias(2)
+        residual_on_tensor(2, 0, tpp.tile([P, HALF], F32, name="w_bank"), True)
+        scale_w(7, 0)
+        quantize_w(6)
+        for m in (2, 0):
+            multiply(6, m)
+        quantize_w(7)
+        for m in (2, 0):
+            multiply(7, m)
+        for u in (6, 7):
+            multiply(u, 1)
+        residual_on_tensor(0, 0, accp.tile([P, HALF], F32, name="h_bank", tag="early0"))
+        residual_on_tensor(2, 1, tpp.tile([P, HALF], F32, name="w_bank"), True)
+        gain_p(2, 0)
+        gain_p(1, 0)
         square_p(2, 1)
         first_root(2)
-        for m in (1, 0, 2):
-            first_norm(m)
-            second_root(m)
-        for m in (1, 0, 2):
-            second_norm(m)
+        gain_p(0, 1)
+        gain_p(2, 1)
+        square_p(1, 1)
+        first_root(1)
+        diagonal(2)
+        for hf in range(HALVES):
+            first_norm_on_tensor(2, hf)
+        first_norm(1, 0)
+        square_p(0, 1)
+        first_root(0)
+        square_z(1, 0)
+        gain_p(1, 1)
+        first_norm(1, 1)
+        square_z(2, 0)
+        square_z(1, 1)
+        square_z(2, 1)
+        for hf in range(HALVES):
+            first_norm(0, hf)
+            square_z(0, hf)
+        for m in (1, 2, 0):
+            for hf in range(HALVES):
+                second_norm(m, hf)

@@ -229,9 +229,7 @@ def tile_recursivemamba130m_pb_kernel(
             nc.gpsimd.tensor_tensor(out=h_sb[m][:, cols], in0=x_sb[m][:, cols], in1=step_bc[:, cols], op=ALU.add)
 
         def first_bias(m):
-            nc.gpsimd.tensor_scalar(
-                out=bias_a[m][:], in0=ss_p[m][0][:], scalar1=1.0 / D, scalar2=EPS, op0=ALU.mult, op1=ALU.add
-            )
+            nc.scalar.activation(out=bias_a[m][:], in_=ss_p[m][0][:], func=ACT.Identity, bias=eps_col[:], scale=1.0 / D)
 
         def first_root(m):
             nc.scalar.activation(
@@ -261,14 +259,18 @@ def tile_recursivemamba130m_pb_kernel(
         def square_z(m, hf):
             junk = stream.tile([P, HALF], F32, name="junk_p")
             nc.scalar.activation(out=junk[:], in_=z_of(m, hf), func=ACT.Square, accum_out=ss_z[m][hf][:])
-            if hf == 0:
-                nc.gpsimd.tensor_scalar(
-                    out=bias_z[m][:], in0=ss_z[m][0][:], scalar1=1.0 / D, scalar2=EPS, op0=ALU.mult, op1=ALU.add
-                )
-            else:
-                nc.scalar.activation(
-                    out=r2[m][:], in_=ss_z[m][1][:], func=ACT.Abs_reciprocal_sqrt, bias=bias_z[m][:], scale=1.0 / D
-                )
+
+        def second_bias(m):
+            nc.scalar.activation(out=bias_z[m][:], in_=ss_z[m][0][:], func=ACT.Identity, bias=eps_col[:], scale=1.0 / D)
+
+        def second_root(m, bias):
+            nc.scalar.activation(
+                out=r2[m][:], in_=ss_z[m][1][:], func=ACT.Abs_reciprocal_sqrt, bias=bias[:], scale=1.0 / D
+            )
+
+        def square_whole(m):
+            junk = keep.tile([P, D], F32, name="junk_z")
+            nc.scalar.activation(out=junk[:], in_=z_sb[m][:], func=ACT.Square, accum_out=ss_z[m][1][:])
 
         def second_norm(m, hf):
             cols = slice(hf * HALF, (hf + 1) * HALF)
@@ -327,6 +329,8 @@ def tile_recursivemamba130m_pb_kernel(
                 scale_w_on_scalar(7, 1)
                 square_p(1, 0)
                 square_p(2, 0)
+                for m in range(M_TILES):
+                    first_bias(m)
             scale_w(u, 1)
             if u == 0:
                 widen(2, (0, 1, 2), "scalar")
@@ -347,12 +351,12 @@ def tile_recursivemamba130m_pb_kernel(
                     empty_y(u, b)
             if 1 <= u <= M_TILES:
                 quantize_y(u - 1)
-            if u >= 1:
+            if 1 <= u <= 5:
                 gpsimd_waits_for(y_codes[u - 1] if u <= M_TILES else w_codes[u - 1])
             if u in (1, 2):
                 widen(u + 3, (3,), "gpsimd")
-            if 3 <= u <= 5:
-                residual_on_gpsimd(*((1, 0), (1, 1), (0, 1))[u - 3])
+            if u in (3, 4):
+                residual_on_gpsimd(1, u - 3)
             for v in range(u):
                 for m in range(min(u, M_TILES)):
                     if v == u - 1 or m == u - 1:
@@ -361,11 +365,7 @@ def tile_recursivemamba130m_pb_kernel(
                 copy_p(0, 0)
                 square_p(0, 0)
             if u == 5:
-                first_bias(0)
-            if u == 6:
                 gain_p_on_gpsimd(0, 0)
-                first_bias(1)
-                first_bias(2)
         residual_on_tensor(2, 0, tpp.tile([P, HALF], F32, name="w_bank"), True)
         scale_w(7, 0)
         quantize_w(6)
@@ -378,6 +378,8 @@ def tile_recursivemamba130m_pb_kernel(
             multiply(u, 1)
         residual_on_tensor(0, 0, accp.tile([P, HALF], F32, name="h_bank", tag="early0"))
         residual_on_tensor(2, 1, tpp.tile([P, HALF], F32, name="w_bank"), True)
+        gpsimd_waits_for(w_codes[7])
+        residual_on_gpsimd(0, 1)
         gain_p(2, 0)
         gain_p(1, 0)
         square_p(2, 1)
@@ -396,11 +398,16 @@ def tile_recursivemamba130m_pb_kernel(
         gain_p(1, 1)
         first_norm(1, 1)
         square_z(2, 0)
+        second_bias(1)
         square_z(1, 1)
+        second_bias(2)
+        second_root(1, bias_z[1])
         square_z(2, 1)
+        second_root(2, bias_z[2])
         for hf in range(HALVES):
             first_norm(0, hf)
-            square_z(0, hf)
+        square_whole(0)
+        second_root(0, eps_col)
         for m in (1, 2, 0):
             for hf in range(HALVES):
                 second_norm(m, hf)

@@ -279,6 +279,27 @@ def tile_recursivemamba130m_pb_kernel(
             )
             nc.sync.dma_start(out=out2[m * P : (m + 1) * P, cols], in_=res_sb[m][:, cols])
 
+        def scale_w_by_planes(u, b):
+            g = u % PASSES
+            w_planes[(u, b)] = keep.tile([P, 4, 256], BF16, name="w_planes%d_%d" % (u, b))
+            planes_in = w_banks[(u, b)][:].bitcast(BF16).rearrange("p (u r e) -> p u r e", u=2, e=2)
+            for t in range(4):
+                nc.scalar.activation(
+                    out=w_planes[(u, b)][:, t, :], in_=planes_in[:, t // 2, :, t % 2], func=ACT.Copy,
+                    scale=scale4[:, 8 * g + t : 8 * g + t + 1],
+                )
+
+        w_planes = {}
+
+        def interleave_w(u, b):
+            if u not in w_grouped:
+                w_grouped[u] = stream.tile([P, 4 * HALF], BF16, name="w_grouped", align_bytes=64, bufs=4)
+            nc.gpsimd.tensor_scalar(
+                out=w_grouped[u][:, b * 1024 : (b + 1) * 1024].rearrange("p (r t) -> p r t", t=4),
+                in0=w_planes[(u, b)][:].rearrange("p t r -> p r t"),
+                scalar1=1.0, scalar2=0.0, op0=ALU.mult, op1=ALU.add,
+            )
+
         half_banks = {}
 
         def turn_half(u, j):
@@ -316,33 +337,37 @@ def tile_recursivemamba130m_pb_kernel(
         turn_half(0, 0)
         turn_half(0, 1)
         turn_w(0, 1)
-        widen(1, (0, 1, 2, 3), "scalar")
-        for u in range(UNITS - 1):
+        widen(1, (0, 1, 2), "scalar")
+        widen(1, (3,), "gpsimd")
+        for u in range(6):
             if u == 0:
                 scale_half(0, 0)
                 scale_half(0, 1)
             else:
                 scale_w(u, 0)
             turn_w(u + 1, 0)
-            if u == 5:
-                turn_w(7, 1, accp.tile([P, HALF], F32, name="s_bank", tag="early0"))
-                scale_w_on_scalar(7, 1)
-                square_p(1, 0)
-                square_p(2, 0)
-                for m in range(M_TILES):
-                    first_bias(m)
+            if u == 4:
+                turn_w(6, 1, accp.tile([P, HALF], F32, name="s_bank", tag="late0"))
             scale_w(u, 1)
             if u == 0:
                 widen(2, (0, 1, 2), "scalar")
                 widen(2, (3,), "gpsimd")
-                widen(3, (3,), "gpsimd")
             elif u <= 3:
-                widen(u + 2, (0, 1, 2), "scalar")
-            elif u == 4:
-                widen(6, (0, 1, 2, 3), "scalar")
-                widen(7, (2, 3, 0, 1), "scalar")
-            if u < 6:
+                widen(u + 2, (0, 1, 2) if u < 3 else (0, 1, 2, 3), "scalar")
+            if u == 3:
+                widen(6, (2, 3), "scalar")
+            if u == 4:
+                widen(6, (0, 1), "scalar")
+                widen(7, (2, 3), "scalar")
+                scale_w_by_planes(6, 1)
+                widen(7, (0, 1), "scalar")
+            if u < 5:
                 turn_w(u + 1, 1)
+            else:
+                turn_w(7, 0)
+            if u == 4:
+                turn_w(7, 1, accp.tile([P, HALF], F32, name="s_bank", tag="late1"))
+                scale_w_on_scalar(7, 1)
             if u >= 1:
                 quantize_w(u - 1)
             if u < M_TILES:
@@ -351,23 +376,29 @@ def tile_recursivemamba130m_pb_kernel(
                     empty_y(u, b)
             if 1 <= u <= M_TILES:
                 quantize_y(u - 1)
-            if 1 <= u <= 5:
+            if 1 <= u:
                 gpsimd_waits_for(y_codes[u - 1] if u <= M_TILES else w_codes[u - 1])
             if u in (1, 2):
-                widen(u + 3, (3,), "gpsimd")
+                widen(u + 2, (3,), "gpsimd")
             if u in (3, 4):
                 residual_on_gpsimd(1, u - 3)
             for v in range(u):
                 for m in range(min(u, M_TILES)):
-                    if v == u - 1 or m == u - 1:
+                    if (v == u - 1 or m == u - 1) and (v, m) != (4, 1):
                         multiply(v, m)
-            if u == 4:
-                copy_p(0, 0)
-                square_p(0, 0)
             if u == 5:
-                gain_p_on_gpsimd(0, 0)
+                interleave_w(6, 1)
+        scale_w(6, 0)
         residual_on_tensor(2, 0, tpp.tile([P, HALF], F32, name="w_bank"), True)
         scale_w(7, 0)
+        residual_on_tensor(2, 1, tpp.tile([P, HALF], F32, name="w_bank"), True)
+        for m in range(M_TILES):
+            square_p(m, 0)
+        for m in range(M_TILES):
+            first_bias(m)
+        quantize_w(5)
+        for u, m in ((5, 2), (5, 0), (4, 1), (5, 1)):
+            multiply(u, m)
         quantize_w(6)
         for m in (2, 0):
             multiply(6, m)
@@ -376,12 +407,11 @@ def tile_recursivemamba130m_pb_kernel(
             multiply(7, m)
         for u in (6, 7):
             multiply(u, 1)
+        for m in range(M_TILES):
+            gain_p(m, 0)
         residual_on_tensor(0, 0, accp.tile([P, HALF], F32, name="h_bank", tag="early0"))
-        residual_on_tensor(2, 1, tpp.tile([P, HALF], F32, name="w_bank"), True)
         gpsimd_waits_for(w_codes[7])
         residual_on_gpsimd(0, 1)
-        gain_p(2, 0)
-        gain_p(1, 0)
         square_p(2, 1)
         first_root(2)
         gain_p(0, 1)

@@ -339,34 +339,37 @@ def tile_recursivemamba130m_pb_kernel(
         turn_w(0, 1)
         widen(1, (0, 1, 2), "scalar")
         widen(1, (3,), "gpsimd")
-        for u in range(6):
+        for u in range(5):
             if u == 0:
                 scale_half(0, 0)
                 scale_half(0, 1)
             else:
                 scale_w(u, 0)
             turn_w(u + 1, 0)
-            if u == 4:
-                turn_w(6, 1, accp.tile([P, HALF], F32, name="s_bank", tag="late0"))
             scale_w(u, 1)
             if u == 0:
-                widen(2, (0, 1, 2), "scalar")
-                widen(2, (3,), "gpsimd")
-            elif u <= 3:
-                widen(u + 2, (0, 1, 2) if u < 3 else (0, 1, 2, 3), "scalar")
+                widen(2, (0, 1), "scalar")
+                widen(2, (2, 3), "gpsimd")
+            elif u <= 2:
+                widen(u + 2, (0, 1), "scalar")
+            if u == 2:
+                widen(5, (0, 1), "scalar")
+            if u == 3:
+                widen(5, (3,), "scalar")
+                turn_w(5, 1, accp.tile([P, HALF], F32, name="s_bank", tag="late0"))
+            if u < 4:
+                turn_w(u + 1, 1)
             if u == 3:
                 widen(6, (2, 3), "scalar")
-            if u == 4:
-                widen(6, (0, 1), "scalar")
+                scale_w_by_planes(5, 1)
                 widen(7, (2, 3), "scalar")
+                widen(6, (0, 1), "scalar")
+            if u == 4:
+                turn_w(6, 1, accp.tile([P, HALF], F32, name="s_bank", tag="late2"))
+                turn_w(6, 0)
+                turn_w(7, 1, accp.tile([P, HALF], F32, name="s_bank", tag="late1"))
                 scale_w_by_planes(6, 1)
                 widen(7, (0, 1), "scalar")
-            if u < 5:
-                turn_w(u + 1, 1)
-            else:
-                turn_w(7, 0)
-            if u == 4:
-                turn_w(7, 1, accp.tile([P, HALF], F32, name="s_bank", tag="late1"))
                 scale_w_on_scalar(7, 1)
             if u >= 1:
                 quantize_w(u - 1)
@@ -376,39 +379,49 @@ def tile_recursivemamba130m_pb_kernel(
                     empty_y(u, b)
             if 1 <= u <= M_TILES:
                 quantize_y(u - 1)
-            if 1 <= u:
-                gpsimd_waits_for(y_codes[u - 1] if u <= M_TILES else w_codes[u - 1])
+            if u == 2:
+                widen(5, (2,), "vector")
+            if 1 <= u <= 3:
+                gpsimd_waits_for(y_codes[u - 1])
             if u in (1, 2):
-                widen(u + 2, (3,), "gpsimd")
-            if u in (3, 4):
-                residual_on_gpsimd(1, u - 3)
+                widen(u + 2, (2, 3), "gpsimd")
+            if u == 3:
+                residual_on_gpsimd(1, 0)
             for v in range(u):
                 for m in range(min(u, M_TILES)):
-                    if (v == u - 1 or m == u - 1) and (v, m) != (4, 1):
+                    if v == u - 1 or m == u - 1:
                         multiply(v, m)
-            if u == 5:
-                interleave_w(6, 1)
+        quantize_w(4)
+        gpsimd_waits_for(w_codes[4])
+        interleave_w(5, 1)
+        interleave_w(6, 1)
+        residual_on_gpsimd(1, 1)
+        scale_w(5, 0)
+        multiply(4, 0)
+        multiply(4, 2)
+        turn_w(7, 0)
         scale_w(6, 0)
         residual_on_tensor(2, 0, tpp.tile([P, HALF], F32, name="w_bank"), True)
+        gain_p(0, 0)
         scale_w(7, 0)
         residual_on_tensor(2, 1, tpp.tile([P, HALF], F32, name="w_bank"), True)
-        for m in range(M_TILES):
+        for m in (1, 2, 0):
             square_p(m, 0)
         for m in range(M_TILES):
             first_bias(m)
         quantize_w(5)
-        for u, m in ((5, 2), (5, 0), (4, 1), (5, 1)):
-            multiply(u, m)
+        for m in (2, 0):
+            multiply(5, m)
         quantize_w(6)
         for m in (2, 0):
             multiply(6, m)
         quantize_w(7)
         for m in (2, 0):
             multiply(7, m)
-        for u in (6, 7):
+        for u in (4, 5, 6, 7):
             multiply(u, 1)
-        for m in range(M_TILES):
-            gain_p(m, 0)
+        gain_p(1, 0)
+        gain_p(2, 0)
         residual_on_tensor(0, 0, accp.tile([P, HALF], F32, name="h_bank", tag="early0"))
         gpsimd_waits_for(w_codes[7])
         residual_on_gpsimd(0, 1)
@@ -416,28 +429,28 @@ def tile_recursivemamba130m_pb_kernel(
         first_root(2)
         gain_p(0, 1)
         gain_p(2, 1)
-        square_p(1, 1)
-        first_root(1)
         diagonal(2)
         for hf in range(HALVES):
             first_norm_on_tensor(2, hf)
-        first_norm(1, 0)
         square_p(0, 1)
         first_root(0)
-        square_z(1, 0)
+        first_norm(0, 0)
+        first_norm(0, 1)
+        square_p(1, 1)
+        first_root(1)
         gain_p(1, 1)
-        first_norm(1, 1)
+        square_z(0, 0)
+        square_z(0, 1)
+        second_bias(0)
         square_z(2, 0)
-        second_bias(1)
-        square_z(1, 1)
+        second_root(0, bias_z[0])
         second_bias(2)
-        second_root(1, bias_z[1])
         square_z(2, 1)
         second_root(2, bias_z[2])
         for hf in range(HALVES):
-            first_norm(0, hf)
-        square_whole(0)
-        second_root(0, eps_col)
-        for m in (1, 2, 0):
+            first_norm(1, hf)
+        square_whole(1)
+        second_root(1, eps_col)
+        for m in (0, 2, 1):
             for hf in range(HALVES):
                 second_norm(m, hf)

@@ -300,6 +300,9 @@ def tile_recursivemamba130m_pb_kernel(
                 scalar1=1.0, scalar2=0.0, op0=ALU.mult, op1=ALU.add,
             )
 
+        def diagonal_on_scalar(m):
+            nc.scalar.activation(out=diag_r1[:], in_=ident[:], func=ACT.Copy, scale=r1[m][:])
+
         half_banks = {}
 
         def turn_half(u, j):
@@ -348,8 +351,10 @@ def tile_recursivemamba130m_pb_kernel(
             turn_w(u + 1, 0)
             scale_w(u, 1)
             if u == 0:
-                widen(2, (0, 1), "scalar")
-                widen(2, (2, 3), "gpsimd")
+                widen(2, (0, 1, 2), "scalar")
+                widen(3, (2,), "scalar")
+                widen(2, (3,), "gpsimd")
+                widen(3, (3,), "gpsimd")
             elif u <= 2:
                 widen(u + 2, (0, 1), "scalar")
             if u == 2:
@@ -384,7 +389,7 @@ def tile_recursivemamba130m_pb_kernel(
             if 1 <= u <= 3:
                 gpsimd_waits_for(y_codes[u - 1])
             if u in (1, 2):
-                widen(u + 2, (2, 3), "gpsimd")
+                widen(4, (4 - u,), "gpsimd")
             if u == 3:
                 residual_on_gpsimd(1, 0)
             for v in range(u):
@@ -395,7 +400,6 @@ def tile_recursivemamba130m_pb_kernel(
         gpsimd_waits_for(w_codes[4])
         interleave_w(5, 1)
         interleave_w(6, 1)
-        residual_on_gpsimd(1, 1)
         scale_w(5, 0)
         multiply(4, 0)
         multiply(4, 2)
@@ -425,14 +429,15 @@ def tile_recursivemamba130m_pb_kernel(
         residual_on_tensor(0, 0, accp.tile([P, HALF], F32, name="h_bank", tag="early0"))
         gpsimd_waits_for(w_codes[7])
         residual_on_gpsimd(0, 1)
+        residual_on_gpsimd(1, 1)
         square_p(2, 1)
         first_root(2)
         gain_p(0, 1)
         gain_p(2, 1)
-        diagonal(2)
+        square_p(0, 1)
+        diagonal_on_scalar(2)
         for hf in range(HALVES):
             first_norm_on_tensor(2, hf)
-        square_p(0, 1)
         first_root(0)
         first_norm(0, 0)
         first_norm(0, 1)

@@ -303,6 +303,12 @@ def tile_recursivemamba130m_pb_kernel(
         def diagonal_on_scalar(m):
             nc.scalar.activation(out=diag_r1[:], in_=ident[:], func=ACT.Copy, scale=r1[m][:])
 
+        def second_norm_part(m, lo, hi):
+            nc.vector.scalar_tensor_tensor(
+                out=res_sb[m][:, lo:hi], in0=z_sb[m][:, lo:hi], scalar=r2[m][:], in1=w2_bc[:, lo:hi], op0=ALU.mult, op1=ALU.mult
+            )
+            nc.sync.dma_start(out=out2[m * P : (m + 1) * P, lo:hi], in_=res_sb[m][:, lo:hi])
+
         half_banks = {}
 
         def turn_half(u, j):
@@ -367,43 +373,42 @@ def tile_recursivemamba130m_pb_kernel(
             if u == 3:
                 widen(6, (2, 3), "scalar")
                 scale_w_by_planes(5, 1)
-                widen(7, (2, 3), "scalar")
-                widen(6, (0, 1), "scalar")
-            if u == 4:
                 turn_w(6, 1, accp.tile([P, HALF], F32, name="s_bank", tag="late2"))
+                widen(6, (0, 1), "scalar")
+                widen(7, (2, 3), "scalar")
+                scale_w_by_planes(6, 1)
+            if u == 4:
                 turn_w(6, 0)
                 turn_w(7, 1, accp.tile([P, HALF], F32, name="s_bank", tag="late1"))
-                scale_w_by_planes(6, 1)
                 widen(7, (0, 1), "scalar")
                 scale_w_on_scalar(7, 1)
             if u >= 1:
                 quantize_w(u - 1)
-            if u < M_TILES:
-                for b in range(2):
-                    turn_y(u, b)
-                    empty_y(u, b)
-            if 1 <= u <= M_TILES:
-                quantize_y(u - 1)
+            for m, b in (((0, 0),), ((0, 1), (1, 0)), ((1, 1), (2, 0), (2, 1)), (), ())[u]:
+                turn_y(m, b)
+                empty_y(m, b)
+            if u >= 2:
+                quantize_y(u - 2)
             if u == 2:
                 widen(5, (2,), "vector")
             if 1 <= u <= 3:
-                gpsimd_waits_for(y_codes[u - 1])
+                gpsimd_waits_for(y_codes[u - 2] if u > 1 else w_codes[0])
             if u in (1, 2):
                 widen(4, (4 - u,), "gpsimd")
             if u == 3:
-                residual_on_gpsimd(1, 0)
+                residual_on_gpsimd(0, 0)
             for v in range(u):
-                for m in range(min(u, M_TILES)):
-                    if v == u - 1 or m == u - 1:
+                for m in range(u - 1):
+                    if v == u - 1 or m == u - 2:
                         multiply(v, m)
         quantize_w(4)
         gpsimd_waits_for(w_codes[4])
         interleave_w(5, 1)
         interleave_w(6, 1)
         scale_w(5, 0)
+        turn_w(7, 0)
         multiply(4, 0)
         multiply(4, 2)
-        turn_w(7, 0)
         scale_w(6, 0)
         residual_on_tensor(2, 0, tpp.tile([P, HALF], F32, name="w_bank"), True)
         gain_p(0, 0)
@@ -411,7 +416,7 @@ def tile_recursivemamba130m_pb_kernel(
         residual_on_tensor(2, 1, tpp.tile([P, HALF], F32, name="w_bank"), True)
         for m in (1, 2, 0):
             square_p(m, 0)
-        for m in range(M_TILES):
+        for m in (1, 2, 0):
             first_bias(m)
         quantize_w(5)
         for m in (2, 0):
@@ -426,7 +431,7 @@ def tile_recursivemamba130m_pb_kernel(
             multiply(u, 1)
         gain_p(1, 0)
         gain_p(2, 0)
-        residual_on_tensor(0, 0, accp.tile([P, HALF], F32, name="h_bank", tag="early0"))
+        residual_on_tensor(1, 0, accp.tile([P, HALF], F32, name="h_bank", tag="early0"))
         gpsimd_waits_for(w_codes[7])
         residual_on_gpsimd(0, 1)
         residual_on_gpsimd(1, 1)
@@ -456,6 +461,9 @@ def tile_recursivemamba130m_pb_kernel(
             first_norm(1, hf)
         square_whole(1)
         second_root(1, eps_col)
-        for m in (0, 2, 1):
+        for m in (0, 2):
             for hf in range(HALVES):
                 second_norm(m, hf)
+        second_norm(1, 0)
+        second_norm_part(1, 512, 768)
+        second_norm_part(1, 768, 1024)

from contextlib import ExitStack

import concourse.mybir as mybir
from concourse.masks import make_identity

F32 = mybir.dt.float32
BF16 = mybir.dt.bfloat16
U32 = mybir.dt.uint32
U8 = mybir.dt.uint8
FP8 = mybir.dt.float8_e4m3fn
FP8X4 = mybir.dt.float8_e4m3fn_x4
ALU = mybir.AluOpType
ACT = mybir.ActivationFunctionType

L, D, K = 384, 1024, 2048
EPS = 1e-6
FLOPS = 2 * L * D * K

P = 128
K_PASS = 512
PASSES = K // K_PASS
M_TILES = L // P
HALF = 512
HALVES = D // HALF
UNITS = HALVES * PASSES
ROW_TILES = D // P


def tile_recursivemamba130m_pb_kernel(
    tc, y, x, step_emb, out_proj_w_bytes, out_proj_w_scale, mixer_norm_w, loop_norm_w, out
):
    nc = tc.nc
    y2 = y.flatten_outer_dims()
    x2 = x.flatten_outer_dims()
    out2 = out.flatten_outer_dims()

    with ExitStack() as ctx:
        keep = ctx.enter_context(tc.tile_pool(name="keep", bufs=1))
        stream = ctx.enter_context(tc.tile_pool(name="stream", bufs=3))
        accp = ctx.enter_context(tc.psum_pool(name="accp", bufs=1))
        tpp = ctx.enter_context(tc.psum_pool(name="tpp", bufs=2))
        ctx.enter_context(tc.manual_schedule())

        scale4 = keep.tile([P, PASSES * 8], F32, name="scale4")
        scale_view = out_proj_w_scale.rearrange("o (g p t) -> g p (o t)", p=P, t=4)

        def load_scales(g):
            nc.sync.dma_start(out=scale4[:, 8 * g : 8 * g + 4], in_=scale_view[g])

        ident = keep.tile([P, P], F32, name="ident")
        make_identity(nc, ident[:])
        zero_col = keep.tile([P, 1], F32, name="zero_col")
        nc.vector.memset(zero_col[:], 0.0)
        eps_col = keep.tile([P, 1], F32, name="eps_col")
        nc.vector.tensor_scalar(out=eps_col[:], in0=zero_col[:], scalar1=EPS, scalar2=None, op0=ALU.add)
        warm_col = keep.tile([P, 1], F32, name="warm_col")
        nc.scalar.activation(out=warm_col[:], in_=eps_col[:], func=ACT.Abs_reciprocal_sqrt)
        ident_bf = keep.tile([P, P], BF16, name="ident_bf")
        make_identity(nc, ident_bf[:])
        ones_bf = keep.tile([P, P], BF16, name="ones_bf")
        nc.vector.memset(ones_bf[:], 1.0)
        step_pad = keep.tile([P, D], BF16, name="step_pad")
        nc.vector.memset(step_pad[:], 0.0)

        w_bytes = [keep.tile([P, K], U8, name="w_bytes%d" % r) for r in range(ROW_TILES)]
        y_sb = [keep.tile([P, K], BF16, name="y_sb%d" % m) for m in range(M_TILES)]
        x_sb = [keep.tile([P, D], BF16, name="x_sb%d" % m) for m in range(M_TILES)]
        step_bc = keep.tile([P, D], BF16, name="step_bc")
        w1_bc = keep.tile([P, D], BF16, name="w1_bc")
        w2_bc = keep.tile([P, D], BF16, name="w2_bc")

        def load_w(r):
            nc.sync.dma_start(out=w_bytes[r][:], in_=out_proj_w_bytes[r * P : (r + 1) * P, :])

        for r in range(4):
            nc.sync.dma_start(out=w_bytes[r][:, :K_PASS], in_=out_proj_w_bytes[r * P : (r + 1) * P, :K_PASS])
        load_scales(0)
        for r in range(4):
            nc.sync.dma_start(out=w_bytes[r][:, K_PASS:], in_=out_proj_w_bytes[r * P : (r + 1) * P, K_PASS:])
        for g in range(1, PASSES):
            load_scales(g)
        for m in range(M_TILES):
            nc.sync.dma_start(out=y_sb[m][:], in_=y2[m * P : (m + 1) * P, :])
        for r in range(4, 8):
            load_w(r)
        nc.sync.dma_start(out=step_pad[0:1, :], in_=step_emb.rearrange("(o d) -> o d", o=1))
        for m in range(M_TILES):
            nc.sync.dma_start(out=x_sb[m][:], in_=x2[m * P : (m + 1) * P, :])
        nc.sync.dma_start(out=step_bc[:], in_=step_emb.partition_broadcast(P))
        nc.sync.dma_start(out=w1_bc[:], in_=mixer_norm_w.partition_broadcast(P))
        nc.sync.dma_start(out=w2_bc[:], in_=loop_norm_w.partition_broadcast(P))

        y_codes = [keep.tile([P, PASSES * P], U32, name="y_codes%d" % m, align_bytes=64) for m in range(M_TILES)]
        y_scales = [keep.tile([P, PASSES * P], U8, name="y_scales%d" % m, align_bytes=64) for m in range(M_TILES)]
        w_codes = [keep.tile([P, HALF], U32, name="w_codes%d" % u, align_bytes=64) for u in range(UNITS)]
        w_scales = [keep.tile([P, HALF], U8, name="w_scales%d" % u, align_bytes=64) for u in range(UNITS)]
        h_sb = [keep.tile([P, D], F32, name="h_sb%d" % m) for m in range(2)]
        h_banks = {}
        diag_r1 = keep.tile([P, P], F32, name="diag_r1")
        pw_sb = [keep.tile([P, D], F32, name="pw_sb%d" % m) for m in range(M_TILES)]
        z_sb = [keep.tile([P, D], F32, name="z_sb%d" % m) for m in range(M_TILES)]
        res_sb = [keep.tile([P, D], F32, name="res_sb%d" % m) for m in range(M_TILES)]
        ss_p = [[keep.tile([P, 1], F32, name="ss_p%d_%d" % (m, hf)) for hf in range(HALVES)] for m in range(M_TILES)]
        bias_a = [keep.tile([P, 1], F32, name="bias_a%d" % m) for m in range(M_TILES)]
        r1 = [keep.tile([P, 1], F32, name="r1_%d" % m) for m in range(M_TILES)]
        ss_z = [[keep.tile([P, 1], F32, name="ss_z%d_%d" % (m, hf)) for hf in range(HALVES)] for m in range(M_TILES)]
        bias_z = [keep.tile([P, 1], F32, name="bias_z%d" % m) for m in range(M_TILES)]
        r2 = [keep.tile([P, 1], F32, name="r2_%d" % m) for m in range(M_TILES)]
        acc = {}

        def turn_bank(bank, word_blocks):
            for jj in range(2):
                for uu in range(2):
                    nc.tensor.transpose(
                        bank[:, uu * 256 + jj * P : uu * 256 + (jj + 1) * P], word_blocks[jj][:, uu : 2 * P : 2], ident[:]
                    )

        y_grouped = [stream.tile([P, K], BF16, name="y_grouped", align_bytes=64) for m in range(M_TILES)]
        y_banks = {}

        def turn_y(m, b):
            bank = accp.tile([P, 512], F32, name="y_bank", tag="late%d" % ((2 * m + b) % 3))
            words = y_sb[m][:].bitcast(F32)
            turn_bank(bank, [words[:, (2 * b + jj) * 256 : (2 * b + jj + 1) * 256] for jj in range(2)])
            y_banks[(m, b)] = bank

        def empty_y(m, b):
            nc.scalar.copy(
                out=y_grouped[m][:].bitcast(F32)[:, b * 512 : (b + 1) * 512].rearrange("p (r u) -> p r u", u=2),
                in_=y_banks[(m, b)][:].rearrange("p (u r) -> p r u", u=2),
            )

        def quantize_y(m):
            nc.vector.quantize_mx(out=y_codes[m][:].bitcast(FP8X4), scales=y_scales[m][:], in_=y_grouped[m][:])

        w_wide = {}
        w_banks = {}
        w_grouped = {}

        def widen(u, pieces, engine):
            hf, g = divmod(u, PASSES)
            if u not in w_wide:
                w_wide[u] = stream.tile([P, 4, K_PASS], BF16, name="w_wide", bufs=4)
            for j in pieces:
                src = w_bytes[4 * hf + j][:, g * K_PASS : (g + 1) * K_PASS].bitcast(FP8)
                if engine == "vector":
                    nc.vector.tensor_copy(out=w_wide[u][:, j, :], in_=src)
                elif engine == "gpsimd":
                    nc.gpsimd.tensor_copy(out=w_wide[u][:, j, :], in_=src)
                else:
                    nc.scalar.copy(out=w_wide[u][:, j, :], in_=src)

        g_sync = keep.tile([P, 1], U32, name="g_sync")

        def gpsimd_waits_for(codes):
            nc.gpsimd.tensor_copy(out=g_sync[:], in_=codes[:, 0:1])

        def turn_w(u, b, bank=None):
            if bank is None:
                bank = tpp.tile([P, 512], F32, name="w_bank")
            turn_bank(bank, [w_wide[u][:, 2 * b + jj, :].bitcast(F32) for jj in range(2)])
            w_banks[(u, b)] = bank

        def scale_w(u, b):
            g = u % PASSES
            if u not in w_grouped:
                w_grouped[u] = stream.tile([P, 4 * HALF], BF16, name="w_grouped", align_bytes=64, bufs=4)
            nc.vector.tensor_tensor(
                out=w_grouped[u][:, b * 1024 : (b + 1) * 1024].rearrange("p (r u e) -> p r u e", u=2, e=2),
                in0=w_banks[(u, b)][:].bitcast(BF16).rearrange("p (u r e) -> p r u e", u=2, e=2),
                in1=scale4[:, 8 * g : 8 * g + 4].rearrange("p (u e) -> p u e", u=2).unsqueeze(1).to_broadcast([P, 256, 2, 2]),
                op=ALU.mult,
            )

        def scale_w_on_scalar(u, b):
            g = u % PASSES
            if u not in w_grouped:
                w_grouped[u] = stream.tile([P, 4 * HALF], BF16, name="w_grouped", align_bytes=64, bufs=4)
            planes_out = w_grouped[u][:, b * 1024 : (b + 1) * 1024].rearrange("p (r t) -> p r t", t=4)
            planes_in = w_banks[(u, b)][:].bitcast(BF16).rearrange("p (u r e) -> p u r e", u=2, e=2)
            for t in range(4):
                nc.scalar.activation(
                    out=planes_out[:, :, t], in_=planes_in[:, t // 2, :, t % 2], func=ACT.Copy,
                    scale=scale4[:, 8 * g + t : 8 * g + t + 1],
                )

        def quantize_w(u):
            nc.vector.quantize_mx(out=w_codes[u][:].bitcast(FP8X4), scales=w_scales[u][:], in_=w_grouped[u][:])

        def multiply(u, m):
            hf, g = divmod(u, PASSES)
            if g == 0:
                acc[(m, hf)] = accp.tile([P, HALF], F32, name="acc", tag=("early%d" if hf == 0 else "late%d") % m)
            nc.tensor.matmul_mx(
                out=acc[(m, hf)][:],
                lhsT=y_codes[m][:, g * P : (g + 1) * P].bitcast(FP8X4),
                lhsT_scale=y_scales[m][:, g * P : (g + 1) * P],
                rhs=w_codes[u][:].bitcast(FP8X4),
                rhs_scale=w_scales[u][:],
                start=(g == 0),
                stop=(g == PASSES - 1),
            )

        def residual_on_tensor(m, hf, bank, more=False):
            cols = slice(hf * HALF, (hf + 1) * HALF)
            nc.tensor.matmul(out=bank[:], lhsT=ident_bf[:], rhs=x_sb[m][:, cols], start=True, stop=False)
            nc.tensor.matmul(out=bank[:], lhsT=ones_bf[:], rhs=step_pad[:, cols], start=False, stop=not more)
            h_banks[(m, hf)] = bank

        def square_p(m, hf):
            junk = stream.tile([P, HALF], F32, name="junk_p")
            nc.scalar.activation(out=junk[:], in_=acc[(m, hf)][:], func=ACT.Square, accum_out=ss_p[m][hf][:])

        p_sb = [keep.tile([P, HALF], F32, name="p_sb%d" % m) for m in range(2)]

        def gain_p_on_gpsimd(m, hf):
            cols = slice(hf * HALF, (hf + 1) * HALF)
            nc.gpsimd.tensor_tensor(out=pw_sb[m][:, cols], in0=p_sb[m][:], in1=w1_bc[:, cols], op=ALU.mult)

        def copy_p(m, hf):
            nc.scalar.copy(out=p_sb[m][:], in_=acc[(m, hf)][:])

        def gain_p(m, hf):
            cols = slice(hf * HALF, (hf + 1) * HALF)
            nc.vector.tensor_tensor(out=pw_sb[m][:, cols], in0=acc[(m, hf)][:], in1=w1_bc[:, cols], op=ALU.mult)

        def residual_on_gpsimd(m, hf):
            cols = slice(hf * HALF, (hf + 1) * HALF)
            nc.gpsimd.tensor_tensor(out=h_sb[m][:, cols], in0=x_sb[m][:, cols], in1=step_bc[:, cols], op=ALU.add)

        def first_bias(m):
            nc.scalar.activation(out=bias_a[m][:], in_=ss_p[m][0][:], func=ACT.Identity, bias=eps_col[:], scale=1.0 / D)

        def first_root(m):
            nc.scalar.activation(
                out=r1[m][:], in_=ss_p[m][1][:], func=ACT.Abs_reciprocal_sqrt, bias=bias_a[m][:], scale=1.0 / D
            )

        def first_norm(m, hf):
            cols = slice(hf * HALF, (hf + 1) * HALF)
            h = h_banks[(m, hf)][:] if (m, hf) in h_banks else h_sb[m][:, cols]
            nc.vector.scalar_tensor_tensor(
                out=z_sb[m][:, cols], in0=pw_sb[m][:, cols], scalar=r1[m][:], in1=h, op0=ALU.mult, op1=ALU.add
            )

        def diagonal(m):
            nc.vector.tensor_scalar(out=diag_r1[:], in0=ident[:], scalar1=r1[m][:], scalar2=None, op0=ALU.mult)

        def first_norm_on_tensor(m, hf):
            cols = slice(hf * HALF, (hf + 1) * HALF)
            nc.tensor.matmul(
                out=h_banks[(m, hf)][:], lhsT=diag_r1[:], rhs=pw_sb[m][:, cols], start=False, stop=True
            )

        def z_of(m, hf):
            cols = slice(hf * HALF, (hf + 1) * HALF)
            return h_banks[(m, hf)][:] if m == 2 else z_sb[m][:, cols]

        def square_z(m, hf):
            junk = stream.tile([P, HALF], F32, name="junk_p")
            nc.scalar.activation(out=junk[:], in_=z_of(m, hf), func=ACT.Square, accum_out=ss_z[m][hf][:])

        def second_bias(m):
            nc.scalar.activation(out=bias_z[m][:], in_=ss_z[m][0][:], func=ACT.Identity, bias=eps_col[:], scale=1.0 / D)

        def second_root(m, bias):
            nc.scalar.activation(
                out=r2[m][:], in_=ss_z[m][1][:], func=ACT.Abs_reciprocal_sqrt, bias=bias[:], scale=1.0 / D
            )

        def square_whole(m):
            junk = keep.tile([P, D], F32, name="junk_z")
            nc.scalar.activation(out=junk[:], in_=z_sb[m][:], func=ACT.Square, accum_out=ss_z[m][1][:])

        def second_norm(m, hf):
            cols = slice(hf * HALF, (hf + 1) * HALF)
            nc.vector.scalar_tensor_tensor(
                out=res_sb[m][:, cols], in0=z_of(m, hf), scalar=r2[m][:], in1=w2_bc[:, cols], op0=ALU.mult, op1=ALU.mult
            )
            nc.sync.dma_start(out=out2[m * P : (m + 1) * P, cols], in_=res_sb[m][:, cols])

        def scale_w_by_planes(u, b):
            g = u % PASSES
            w_planes[(u, b)] = keep.tile([P, 4, 256], BF16, name="w_planes%d_%d" % (u, b))
            planes_in = w_banks[(u, b)][:].bitcast(BF16).rearrange("p (u r e) -> p u r e", u=2, e=2)
            for t in range(4):
                nc.scalar.activation(
                    out=w_planes[(u, b)][:, t, :], in_=planes_in[:, t // 2, :, t % 2], func=ACT.Copy,
                    scale=scale4[:, 8 * g + t : 8 * g + t + 1],
                )

        w_planes = {}

        def interleave_w(u, b):
            if u not in w_grouped:
                w_grouped[u] = stream.tile([P, 4 * HALF], BF16, name="w_grouped", align_bytes=64, bufs=4)
            nc.gpsimd.tensor_scalar(
                out=w_grouped[u][:, b * 1024 : (b + 1) * 1024].rearrange("p (r t) -> p r t", t=4),
                in0=w_planes[(u, b)][:].rearrange("p t r -> p r t"),
                scalar1=1.0, scalar2=0.0, op0=ALU.mult, op1=ALU.add,
            )

        def diagonal_on_scalar(m):
            nc.scalar.activation(out=diag_r1[:], in_=ident[:], func=ACT.Copy, scale=r1[m][:])

        def second_norm_part(m, lo, hi):
            nc.vector.scalar_tensor_tensor(
                out=res_sb[m][:, lo:hi], in0=z_sb[m][:, lo:hi], scalar=r2[m][:], in1=w2_bc[:, lo:hi], op0=ALU.mult, op1=ALU.mult
            )
            nc.sync.dma_start(out=out2[m * P : (m + 1) * P, lo:hi], in_=res_sb[m][:, lo:hi])

        half_banks = {}

        def turn_half(u, j):
            bank = accp.tile([P, 256], F32, name="half_bank", tag="early%d" % j)
            for uu in range(2):
                nc.tensor.transpose(
                    bank[:, uu * P : (uu + 1) * P], w_wide[u][:, j, :].bitcast(F32)[:, uu : 2 * P : 2], ident[:]
                )
            half_banks[(u, j)] = bank

        def scale_half(u, j):
            g = u % PASSES
            if u not in w_grouped:
                w_grouped[u] = stream.tile([P, 4 * HALF], BF16, name="w_grouped", align_bytes=64, bufs=4)
            nc.vector.tensor_tensor(
                out=w_grouped[u][:, j * 512 : (j + 1) * 512].rearrange("p (r u e) -> p r u e", u=2, e=2),
                in0=half_banks[(u, j)][:].bitcast(BF16).rearrange("p (u r e) -> p r u e", u=2, e=2),
                in1=scale4[:, 8 * g : 8 * g + 4].rearrange("p (u e) -> p u e", u=2).unsqueeze(1).to_broadcast([P, P, 2, 2]),
                op=ALU.mult,
            )

        def gain_z(m, hf):
            cols = slice(hf * HALF, (hf + 1) * HALF)
            nc.vector.tensor_tensor(out=z2_sb[:], in0=z_of(m, hf), in1=w2_bc[:, cols], op=ALU.mult)

        z2_sb = keep.tile([P, HALF], F32, name="z2_sb")

        def second_norm_on_scalar(m, hf):
            cols = slice(hf * HALF, (hf + 1) * HALF)
            nc.scalar.activation(out=res_sb[m][:, cols], in_=z2_sb[:], func=ACT.Copy, scale=r2[m][:])
            nc.sync.dma_start(out=out2[m * P : (m + 1) * P, cols], in_=res_sb[m][:, cols])

        widen(0, (0, 1, 2), "vector")
        widen(0, (3,), "scalar")
        turn_half(0, 0)
        turn_half(0, 1)
        turn_w(0, 1)
        widen(1, (0, 1, 2), "scalar")
        widen(1, (3,), "gpsimd")
        for u in range(5):
            if u == 0:
                scale_half(0, 0)
                scale_half(0, 1)
            else:
                scale_w(u, 0)
            turn_w(u + 1, 0)
            scale_w(u, 1)
            if u == 0:
                widen(2, (0, 1, 2), "scalar")
                widen(3, (2,), "scalar")
                widen(2, (3,), "gpsimd")
                widen(3, (3,), "gpsimd")
            elif u <= 2:
                widen(u + 2, (0, 1), "scalar")
            if u == 2:
                widen(5, (0, 1), "scalar")
            if u == 3:
                widen(5, (3,), "scalar")
                turn_w(5, 1, accp.tile([P, HALF], F32, name="s_bank", tag="late0"))
            if u < 4:
                turn_w(u + 1, 1)
            if u == 3:
                widen(6, (2, 3), "scalar")
                scale_w_by_planes(5, 1)
                turn_w(6, 1, accp.tile([P, HALF], F32, name="s_bank", tag="late2"))
                widen(6, (0, 1), "scalar")
                widen(7, (2, 3), "scalar")
                scale_w_by_planes(6, 1)
            if u == 4:
                turn_w(6, 0)
                turn_w(7, 1, accp.tile([P, HALF], F32, name="s_bank", tag="late1"))
                widen(7, (0, 1), "scalar")
                scale_w_on_scalar(7, 1)
            if u >= 1:
                quantize_w(u - 1)
            for m, b in (((0, 0),), ((0, 1), (1, 0)), ((1, 1), (2, 0), (2, 1)), (), ())[u]:
                turn_y(m, b)
                empty_y(m, b)
            if u >= 2:
                quantize_y(u - 2)
            if u == 2:
                widen(5, (2,), "vector")
            if 1 <= u <= 3:
                gpsimd_waits_for(y_codes[u - 2] if u > 1 else w_codes[0])
            if u in (1, 2):
                widen(4, (4 - u,), "gpsimd")
            if u == 3:
                residual_on_gpsimd(0, 0)
            for v in range(u):
                for m in range(u - 1):
                    if v == u - 1 or m == u - 2:
                        multiply(v, m)
        quantize_w(4)
        gpsimd_waits_for(w_codes[4])
        interleave_w(5, 1)
        interleave_w(6, 1)
        scale_w(5, 0)
        turn_w(7, 0)
        multiply(4, 0)
        multiply(4, 2)
        scale_w(6, 0)
        residual_on_tensor(2, 0, tpp.tile([P, HALF], F32, name="w_bank"), True)
        gain_p(0, 0)
        scale_w(7, 0)
        residual_on_tensor(2, 1, tpp.tile([P, HALF], F32, name="w_bank"), True)
        for m in (1, 2, 0):
            square_p(m, 0)
        for m in (1, 2, 0):
            first_bias(m)
        quantize_w(5)
        for m in (2, 0):
            multiply(5, m)
        quantize_w(6)
        for m in (2, 0):
            multiply(6, m)
        quantize_w(7)
        for m in (2, 0):
            multiply(7, m)
        for u in (4, 5, 6, 7):
            multiply(u, 1)
        gain_p(1, 0)
        gain_p(2, 0)
        residual_on_tensor(1, 0, accp.tile([P, HALF], F32, name="h_bank", tag="early0"))
        gpsimd_waits_for(w_codes[7])
        residual_on_gpsimd(0, 1)
        residual_on_gpsimd(1, 1)
        square_p(2, 1)
        first_root(2)
        gain_p(0, 1)
        gain_p(2, 1)
        square_p(0, 1)
        diagonal_on_scalar(2)
        for hf in range(HALVES):
            first_norm_on_tensor(2, hf)
        first_root(0)
        first_norm(0, 0)
        first_norm(0, 1)
        square_p(1, 1)
        first_root(1)
        gain_p(1, 1)
        square_z(0, 0)
        square_z(0, 1)
        second_bias(0)
        square_z(2, 0)
        second_root(0, bias_z[0])
        second_bias(2)
        square_z(2, 1)
        second_root(2, bias_z[2])
        for hf in range(HALVES):
            first_norm(1, hf)
        square_whole(1)
        second_root(1, eps_col)
        for m in (0, 2):
            for hf in range(HALVES):
                second_norm(m, hf)
        second_norm(1, 0)
        second_norm_part(1, 512, 768)
        second_norm_part(1, 768, 1024)
